import numpy as np
import ml_dtypes


def mxq(x, axis, fmt="e4m3"):
    dtype, down = {"e4m3": (ml_dtypes.float8_e4m3fn, 7), "e5m2": (ml_dtypes.float8_e5m2, 14)}[fmt]
    v = np.moveaxis(np.asarray(x, np.float32).astype(ml_dtypes.bfloat16).astype(np.float64), axis, -1)
    blocks = v.reshape(v.shape[:-1] + (-1, 32))
    amax = np.abs(blocks).max(-1, keepdims=True)
    byte = np.maximum(np.where(amax > 0, np.frexp(amax)[1] - 1 + 127, 0) - down, 1)
    scale = np.exp2(byte - 127.0)
    codes = (blocks / scale).astype(np.float32).astype(dtype).astype(np.float64)
    return np.moveaxis((codes * scale).reshape(v.shape), -1, axis)


WIDE = False


def mx_kscale(k):
    if not WIDE:
        return np.ones(k)
    levels = np.array([10, -10, 5, -5, 0])
    a = np.random.permutation(np.resize(levels, k // 512 * 4)).reshape(k // 512, 4)
    idx = np.arange(k)
    return np.exp2(a[idx // 512, idx % 128 // 32])


BF16 = ml_dtypes.bfloat16


def bf(x):
    return np.asarray(x, np.float32).astype(BF16)


def f64(x):
    return np.asarray(x).astype(np.float64)


E2M1 = np.array([0.0, 0.5, 1.0, 1.5, 2.0, 3.0, 4.0, 6.0, -0.0, -0.5, -1.0, -1.5, -2.0, -3.0, -4.0, -6.0])


def pack_weight(w, fmt):
    k, n = w.shape
    w = f64(bf(w)).reshape(k // 32, 32, n)
    amax = np.abs(w).max(1)
    if fmt == "e4m3":
        byte = np.frexp(amax)[1] - 1 + 127 - 7
    else:
        mant, ex = np.frexp(amax / 6.0)
        byte = np.where(mant > 0.5, ex, ex - 1) + 127
    byte = np.clip(np.where(amax > 0, byte, 1), 1, 254)
    scaled = (w * np.exp2(127.0 - byte)[:, None, :]).reshape(k, n).astype(np.float32)
    by_word = np.ascontiguousarray(scaled.reshape(k // 512, 128, 4, n).transpose(0, 1, 3, 2))
    if fmt == "e4m3":
        words = by_word.astype(ml_dtypes.float8_e4m3fn).view(np.uint8)
    else:
        c = by_word.astype(ml_dtypes.float4_e2m1fn).view(np.uint8) & 0xF
        words = c[..., 0::2] | (c[..., 1::2] << 4)
    return np.ascontiguousarray(words), np.ascontiguousarray(byte.astype(np.uint8).reshape(k // 512, 16, n))


def unpack_weight(words, scales, fmt):
    g, p, n, _ = words.shape
    if fmt == "e4m3":
        vals = np.ascontiguousarray(words).view(ml_dtypes.float8_e4m3fn).astype(np.float64)
    else:
        nib = np.empty((g, p, n, 4), np.uint8)
        nib[..., 0::2] = words & 0xF
        nib[..., 1::2] = words >> 4
        vals = E2M1[nib]
    vals = vals * np.repeat(np.exp2(scales.astype(np.float64) - 127.0), 8, axis=1)[..., None]
    return vals.transpose(0, 1, 3, 2).reshape(g * 512, n)


B, C, T, H, W, AT, AF = 1, 512, 16, 14, 14, 64, 128
D = C // 2
C2 = 2 * C
NKV = AT * AF
REP, REM = AT // T, AT % T
QS = np.sqrt(2.0 / np.sqrt(D))
FMT = "e4m3"


def setup_inputs():
    s = mx_kscale(C2)
    sa, sv = s[:C], s[C:]
    m = np.random.standard_normal((B, C, T))[..., None, None]
    v = bf((np.random.standard_normal((B, C, T, H, W)) + 0.7 * m) * sv[None, :, None, None, None])
    a = bf(np.random.standard_normal((B, C, AT, AF)) * sa[None, :, None, None])
    Wp = np.random.standard_normal((D, C2)) * 0.8 * QS / np.sqrt(C) / s[None, :]
    Wp_words, Wp_scales = pack_weight(np.ascontiguousarray(Wp.T), FMT)
    bp = bf(np.random.standard_normal(D) * 0.1)
    Wg = np.random.standard_normal((D, C2)) / np.sqrt(C) / s[None, :]
    Wg_words, Wg_scales = pack_weight(np.ascontiguousarray(Wg.T), FMT)
    bg = bf(np.random.standard_normal(D) * 0.1)
    return {"v": v,
            "a": a,
            "Wp_words": Wp_words,
            "Wp_scales": Wp_scales,
            "bp": bp,
            "Wg_words": Wg_words,
            "Wg_scales": Wg_scales,
            "bg": bg}


def reference(v, a, Wp_words, Wp_scales, bp, Wg_words, Wg_scales, bg):
    z = f64(v).mean(axis=(3, 4))
    z = np.repeat(z, REP, axis=2)
    if REM:
        z = np.concatenate([z, np.broadcast_to(z[:, :, -1:], (B, C, REM))], axis=2)
    z = np.broadcast_to(z[..., None], (B, C, AT, AF))
    av = np.concatenate([f64(a), z], axis=1).reshape(B, C2, NKV)
    avq = mxq(av, 1, "e4m3")
    phi_av = (unpack_weight(Wp_words, Wp_scales, FMT).T @ avq) + f64(bp)[:, None]
    g_av = (unpack_weight(Wg_words, Wg_scales, FMT).T @ avq) + f64(bg)[:, None]
    return phi_av, g_av.transpose(0, 2, 1)

@@ -1,0 +1,239 @@
+from contextlib import ExitStack
+
+import concourse.mybir as mybir
+
+BF16 = mybir.dt.bfloat16
+F32 = mybir.dt.float32
+I32 = mybir.dt.int32
+U32 = mybir.dt.uint32
+U8 = mybir.dt.uint8
+FP8X4 = mybir.dt.float8_e4m3fn_x4
+ADD = mybir.AluOpType.add
+MULT = mybir.AluOpType.mult
+ACT = mybir.ActivationFunctionType
+
+P = 128
+PACK = 4
+T = 16
+HW = 14 * 14
+N = 8192
+D = 256
+D_TILES = D // P
+STEP = N // T
+ROWS = STEP // P
+A_CHUNK = 2048
+PHI_STEPS = 2
+Z_REP = 4
+T_VECTOR = 10
+T_SCALAR = T - T_VECTOR
+
+FLOPS = 2 * 2 * D * (2 * P * PACK) * N
+
+
+def load_weight(nc, pool, words, scales, label):
+    w_words = pool.tile([P, 2, D], U32, name=label + "_words", align_bytes=64)
+    nc.sync.dma_start(
+        out=w_words[:].bitcast(I32),
+        in_=words.rearrange("g p d j -> p g (d j)").bitcast(I32),
+    )
+    w_scales = pool.tile([P, 2, D], U8, name=label + "_scales", align_bytes=64)
+    nc.vector.memset(w_scales[:].bitcast(I32), 0)
+    for quadrant in range(4):
+        nc.sync.dma_start(
+            out=w_scales[32 * quadrant : 32 * quadrant + 4, :, :].bitcast(I32),
+            in_=scales[:, 4 * quadrant : 4 * quadrant + 4, :].rearrange("g b d -> b g d").bitcast(I32),
+        )
+    return w_words, w_scales
+
+
+def tile_nlgate_pa_t_kernel(tc, v, a, Wp_words, Wp_scales, bp, Wg_words, Wg_scales, bg, out_0, out_1):
+    nc = tc.nc
+    v_rows = v[0].rearrange("(p j) t h w -> p j (t h w)", j=PACK)
+    a_rows = a[0].rearrange("(p j) i f -> p j (i f)", j=PACK)
+    phi_rows = out_0[0].rearrange("(m d) n -> m d n", d=P)
+    g_rows = out_1[0].rearrange("(t q r) d -> t q (r d)", q=P, r=ROWS)
+
+    with ExitStack() as ctx:
+        keep = ctx.enter_context(tc.tile_pool(name="keep", bufs=1))
+        stage = ctx.enter_context(tc.tile_pool(name="stage", bufs=4))
+        psum = ctx.enter_context(tc.psum_pool(name="psum", bufs=4))
+
+        v_sb = []
+        for j in range(PACK):
+            v_j = keep.tile([P, T * HW], BF16, name="v%d" % j)
+            nc.sync.dma_start(out=v_j[:], in_=v_rows[:, j, :])
+            v_sb.append(v_j)
+        wp_words, wp_scales = load_weight(nc, keep, Wp_words, Wp_scales, "wp")
+        wg_words, wg_scales = load_weight(nc, keep, Wg_words, Wg_scales, "wg")
+        a_sb = []
+        for c in range(N // A_CHUNK):
+            a_c = keep.tile([P, PACK, A_CHUNK], BF16, name="a%d" % c)
+            nc.sync.dma_start(out=a_c[:], in_=a_rows[:, :, c * A_CHUNK : (c + 1) * A_CHUNK])
+            a_sb.append(a_c)
+
+        bias_rows = keep.tile([P, 2 * D], BF16)
+        nc.vector.memset(bias_rows[:], 0.0)
+        nc.scalar.dma_start(out=bias_rows[0:1, 0:D], in_=bp.rearrange("(o d) -> o d", o=1))
+        nc.scalar.dma_start(out=bias_rows[0:1, D : 2 * D], in_=bg.rearrange("(o d) -> o d", o=1))
+        ones = keep.tile([P, P], BF16)
+        nc.vector.memset(ones[:], 1.0)
+        bias_ps = psum.tile([P, STEP], F32, tag="phi_ps")
+        nc.tensor.matmul(out=bias_ps[:, 0:D], lhsT=ones[:], rhs=bias_rows[:, D : 2 * D], start=True, stop=True)
+        for m in range(D_TILES):
+            nc.tensor.matmul(
+                out=bias_ps[:, D + 32 * m : D + 32 * (m + 1)],
+                lhsT=bias_rows[:, P * m : P * (m + 1)],
+                rhs=ones[:, 0:32],
+                start=True,
+                stop=True,
+            )
+        bg_sb = keep.tile([P, D], F32)
+        nc.vector.tensor_copy(out=bg_sb[:], in_=bias_ps[:, 0:D])
+        bp_sb = keep.tile([P, D_TILES], F32)
+        nc.vector.tensor_copy(
+            out=bp_sb[:], in_=bias_ps[:, D : D + 32 * D_TILES].rearrange("p (m x) -> p m x", x=32)[:, :, 0]
+        )
+
+        sums_vector = keep.tile([P, PACK, T_VECTOR], F32)
+        sums_scalar = keep.tile([P, PACK, T_SCALAR], F32)
+        for j in range(PACK):
+            nc.vector.tensor_reduce(
+                out=sums_vector[:, j, :],
+                in_=v_sb[j][:, 0 : T_VECTOR * HW].rearrange("p (t s) -> p t s", s=HW),
+                axis=mybir.AxisListType.X,
+                op=ADD,
+            )
+            for i in range(T_SCALAR):
+                unused = stage.tile([P, HW], BF16)
+                nc.scalar.activation(
+                    out=unused[:],
+                    in_=v_sb[j][:, (T_VECTOR + i) * HW : (T_VECTOR + i + 1) * HW],
+                    func=ACT.Copy,
+                    accum_out=sums_scalar[:, j, i : i + 1],
+                )
+        z_grouped = keep.tile([P, T, Z_REP, PACK], BF16, align_bytes=64)
+        nc.vector.tensor_scalar(
+            out=z_grouped[:, 0:T_VECTOR, :, :],
+            in0=sums_vector[:].rearrange("p j t -> p t j").unsqueeze(2).to_broadcast([P, T_VECTOR, Z_REP, PACK]),
+            scalar1=1.0 / HW,
+            scalar2=None,
+            op0=MULT,
+        )
+        nc.vector.tensor_scalar(
+            out=z_grouped[:, T_VECTOR:T, :, :],
+            in0=sums_scalar[:].rearrange("p j t -> p t j").unsqueeze(2).to_broadcast([P, T_SCALAR, Z_REP, PACK]),
+            scalar1=1.0 / HW,
+            scalar2=None,
+            op0=MULT,
+        )
+        z_words = keep.tile([P, T * Z_REP], U32, align_bytes=64)
+        z_scales = keep.tile([P, T * Z_REP], U8, align_bytes=64)
+        nc.vector.memset(z_scales[:].bitcast(I32), 0)
+        nc.vector.quantize_mx(
+            out=z_words[:].bitcast(FP8X4),
+            scales=z_scales[:],
+            in_=z_grouped[:].rearrange("p t x j -> p (t x j)"),
+        )
+
+        z_ps = psum.tile([P, D_TILES, D], F32, tag="g_ps")
+        phi_bias = keep.tile([P, D_TILES, T], F32)
+        for m in range(D_TILES):
+            nc.tensor.matmul_mx(
+                out=z_ps[:, m, 0 : T * Z_REP],
+                lhsT=wp_words[:, 1, P * m : P * (m + 1)].bitcast(FP8X4),
+                lhsT_scale=wp_scales[:, 1, P * m : P * (m + 1)],
+                rhs=z_words[:].bitcast(FP8X4),
+                rhs_scale=z_scales[:],
+                start=True,
+                stop=True,
+            )
+            nc.vector.tensor_scalar(
+                out=phi_bias[:, m, :],
+                in0=z_ps[:, m, 0 : T * Z_REP].rearrange("p (t x) -> p t x", x=Z_REP)[:, :, 0],
+                scalar1=bp_sb[:, m : m + 1],
+                scalar2=None,
+                op0=ADD,
+            )
+
+        zz_words = keep.tile([P, T, P], U32, align_bytes=64)
+        nc.vector.tensor_copy(
+            out=zz_words[:].bitcast(I32),
+            in_=z_words[:].bitcast(I32).rearrange("p (t x) -> p t x", x=Z_REP)[:, :, 0:1].to_broadcast([P, T, P]),
+        )
+        zz_scales = keep.tile([P, T, P], U8, align_bytes=64)
+        nc.vector.tensor_copy(
+            out=zz_scales[:].bitcast(I32),
+            in_=z_scales[:].bitcast(I32).unsqueeze(2).to_broadcast([P, T, P // 4]),
+        )
+
+        phi_st = []
+        for t in range(T):
+            c, u = divmod(t, A_CHUNK // STEP)
+            columns = a_sb[c][:, :, u * STEP : (u + 1) * STEP].rearrange("p j (q r) -> p r q j", r=ROWS)
+            grouped = stage.tile([P, ROWS, P, PACK], BF16, align_bytes=64)
+            nc.vector.tensor_copy(out=grouped[:, 0 : ROWS // 2], in_=columns[:, 0 : ROWS // 2])
+            nc.scalar.copy(out=grouped[:, ROWS // 2 : ROWS], in_=columns[:, ROWS // 2 : ROWS])
+            words = stage.tile([P, ROWS, P], U32, align_bytes=64)
+            scales = stage.tile([P, ROWS, P], U8, align_bytes=64)
+            nc.vector.quantize_mx(
+                out=words[:].rearrange("p r q -> p (r q)").bitcast(FP8X4),
+                scales=scales[:].rearrange("p r q -> p (r q)"),
+                in_=grouped[:].rearrange("p r q j -> p (r q j)"),
+            )
+
+            if t % PHI_STEPS == 0:
+                phi_st = [
+                    stage.tile([P, PHI_STEPS * STEP], F32, name="phi_st%d" % m) for m in range(D_TILES)
+                ]
+            first = (t % PHI_STEPS) * STEP
+            for m in range(D_TILES):
+                phi_ps = psum.tile([P, STEP], F32, tag="phi_ps")
+                nc.tensor.matmul_mx(
+                    out=phi_ps[:],
+                    lhsT=wp_words[:, 0, P * m : P * (m + 1)].bitcast(FP8X4),
+                    lhsT_scale=wp_scales[:, 0, P * m : P * (m + 1)],
+                    rhs=words[:].rearrange("p r q -> p (r q)").bitcast(FP8X4),
+                    rhs_scale=scales[:].rearrange("p r q -> p (r q)"),
+                    start=True,
+                    stop=True,
+                )
+                nc.scalar.activation(
+                    out=phi_st[m][:, first : first + STEP].rearrange("d (q r) -> d q r", r=ROWS),
+                    in_=phi_ps[:].rearrange("d (r q) -> d q r", r=ROWS),
+                    func=ACT.Identity,
+                    bias=phi_bias[:, m, t : t + 1],
+                    scale=1.0,
+                )
+                if t % PHI_STEPS == PHI_STEPS - 1:
+                    last = (t + 1) * STEP
+                    nc.sync.dma_start(out=phi_rows[m, :, last - PHI_STEPS * STEP : last], in_=phi_st[m][:])
+
+            g_st = stage.tile([P, ROWS, D], F32)
+            for r0 in range(0, ROWS, 2):
+                g_ps = psum.tile([P, 2, D], F32, tag="g_ps")
+                for i in range(2):
+                    nc.tensor.matmul_mx(
+                        out=g_ps[:, i, :],
+                        lhsT=words[:, r0 + i, :].bitcast(FP8X4),
+                        lhsT_scale=scales[:, r0 + i, :],
+                        rhs=wg_words[:, 0, :].bitcast(FP8X4),
+                        rhs_scale=wg_scales[:, 0, :],
+                        start=True,
+                        stop=False,
+                    )
+                    nc.tensor.matmul_mx(
+                        out=g_ps[:, i, :],
+                        lhsT=zz_words[:, t, :].bitcast(FP8X4),
+                        lhsT_scale=zz_scales[:, t, :],
+                        rhs=wg_words[:, 1, :].bitcast(FP8X4),
+                        rhs_scale=wg_scales[:, 1, :],
+                        start=False,
+                        stop=True,
+                    )
+                nc.vector.tensor_tensor(
+                    out=g_st[:, r0 : r0 + 2, :],
+                    in0=g_ps[:],
+                    in1=bg_sb[:].unsqueeze(1).to_broadcast([P, 2, D]),
+                    op=ADD,
+                )
+            nc.sync.dma_start(out=g_rows[t], in_=g_st[:].rearrange("q r d -> q (r d)"))

@@ -169,10 +169,11 @@ def tile_nlgate_pa_t_kernel(tc, v, a, Wp_words, Wp_scales, bp, Wg_words, Wg_scal
         phi_st = []
         for t in range(T):
             c, u = divmod(t, A_CHUNK // STEP)
-            columns = a_sb[c][:, :, u * STEP : (u + 1) * STEP].rearrange("p j (q r) -> p r q j", r=ROWS)
+            columns = a_sb[c][:, :, u * STEP : (u + 1) * STEP].rearrange("p j (q r) -> p q j r", r=ROWS)
             grouped = stage.tile([P, ROWS, P, PACK], BF16, align_bytes=64)
-            nc.vector.tensor_copy(out=grouped[:, 0 : ROWS // 2], in_=columns[:, 0 : ROWS // 2])
-            nc.scalar.copy(out=grouped[:, ROWS // 2 : ROWS], in_=columns[:, ROWS // 2 : ROWS])
+            regions = grouped[:].rearrange("p r q j -> p q j r")
+            nc.vector.tensor_copy(out=regions[:, 0 : P // 2], in_=columns[:, 0 : P // 2])
+            nc.scalar.copy(out=regions[:, P // 2 : P], in_=columns[:, P // 2 : P])
             words = stage.tile([P, ROWS, P], U32, align_bytes=64)
             scales = stage.tile([P, ROWS, P], U8, align_bytes=64)
             nc.vector.quantize_mx(

@@ -172,8 +172,11 @@ def tile_nlgate_pa_t_kernel(tc, v, a, Wp_words, Wp_scales, bp, Wg_words, Wg_scal
             columns = a_sb[c][:, :, u * STEP : (u + 1) * STEP].rearrange("p j (q r) -> p q j r", r=ROWS)
             grouped = stage.tile([P, ROWS, P, PACK], BF16, align_bytes=64)
             regions = grouped[:].rearrange("p r q j -> p q j r")
-            nc.vector.tensor_copy(out=regions[:, 0 : P // 2], in_=columns[:, 0 : P // 2])
-            nc.scalar.copy(out=regions[:, P // 2 : P], in_=columns[:, P // 2 : P])
+            nc.gpsimd.tensor_scalar(
+                out=regions[:, P // 2 : P], in0=columns[:, P // 2 : P], scalar1=1.0, scalar2=0.0, op0=MULT, op1=ADD
+            )
+            nc.vector.tensor_copy(out=regions[:, 0 : P // 4], in_=columns[:, 0 : P // 4])
+            nc.scalar.copy(out=regions[:, P // 4 : P // 2], in_=columns[:, P // 4 : P // 2])
             words = stage.tile([P, ROWS, P], U32, align_bytes=64)
             scales = stage.tile([P, ROWS, P], U8, align_bytes=64)
             nc.vector.quantize_mx(

@@ -57,6 +57,7 @@ def tile_nlgate_pa_t_kernel(tc, v, a, Wp_words, Wp_scales, bp, Wg_words, Wg_scal
         keep = ctx.enter_context(tc.tile_pool(name="keep", bufs=1))
         stage = ctx.enter_context(tc.tile_pool(name="stage", bufs=4))
         psum = ctx.enter_context(tc.psum_pool(name="psum", bufs=4))
+        ctx.enter_context(tc.manual_schedule())
 
         v_sb = []
         for j in range(PACK):
@@ -136,7 +137,6 @@ def tile_nlgate_pa_t_kernel(tc, v, a, Wp_words, Wp_scales, bp, Wg_words, Wg_scal
         )
 
         z_ps = psum.tile([P, D_TILES, D], F32, tag="g_ps")
-        phi_bias = keep.tile([P, D_TILES, T], F32)
         for m in range(D_TILES):
             nc.tensor.matmul_mx(
                 out=z_ps[:, m, 0 : T * Z_REP],
@@ -146,13 +146,6 @@ def tile_nlgate_pa_t_kernel(tc, v, a, Wp_words, Wp_scales, bp, Wg_words, Wg_scal
                 rhs_scale=z_scales[:],
                 start=True,
                 stop=True,
-            )
-            nc.vector.tensor_scalar(
-                out=phi_bias[:, m, :],
-                in0=z_ps[:, m, 0 : T * Z_REP].rearrange("p (t x) -> p t x", x=Z_REP)[:, :, 0],
-                scalar1=bp_sb[:, m : m + 1],
-                scalar2=None,
-                op0=ADD,
             )
 
         zz_words = keep.tile([P, T, P], U32, align_bytes=64)
@@ -166,31 +159,45 @@ def tile_nlgate_pa_t_kernel(tc, v, a, Wp_words, Wp_scales, bp, Wg_words, Wg_scal
             in_=z_scales[:].bitcast(I32).unsqueeze(2).to_broadcast([P, T, P // 4]),
         )
 
-        phi_st = []
-        for t in range(T):
+        phi_bias = keep.tile([P, D_TILES, T], F32)
+        for m in range(D_TILES):
+            nc.vector.tensor_scalar(
+                out=phi_bias[:, m, :],
+                in0=z_ps[:, m, 0 : T * Z_REP].rearrange("p (t x) -> p t x", x=Z_REP)[:, :, 0],
+                scalar1=bp_sb[:, m : m + 1],
+                scalar2=None,
+                op0=ADD,
+            )
+
+        grouped_of = {}
+        packed_of = {}
+        phi_st = {}
+
+        def regroup(t):
             c, u = divmod(t, A_CHUNK // STEP)
             columns = a_sb[c][:, :, u * STEP : (u + 1) * STEP].rearrange("p j (q r) -> p q j r", r=ROWS)
             grouped = stage.tile([P, ROWS, P, PACK], BF16, align_bytes=64)
             regions = grouped[:].rearrange("p r q j -> p q j r")
-            nc.gpsimd.tensor_scalar(
-                out=regions[:, P // 2 : P], in0=columns[:, P // 2 : P], scalar1=1.0, scalar2=0.0, op0=MULT, op1=ADD
-            )
-            nc.vector.tensor_copy(out=regions[:, 0 : P // 4], in_=columns[:, 0 : P // 4])
-            nc.scalar.copy(out=regions[:, P // 4 : P // 2], in_=columns[:, P // 4 : P // 2])
+            nc.vector.tensor_copy(out=regions[:, 0 : P // 2], in_=columns[:, 0 : P // 2])
+            nc.scalar.copy(out=regions[:, P // 2 : P], in_=columns[:, P // 2 : P])
+            grouped_of[t] = grouped
+
+        def quantise(t):
             words = stage.tile([P, ROWS, P], U32, align_bytes=64)
             scales = stage.tile([P, ROWS, P], U8, align_bytes=64)
             nc.vector.quantize_mx(
                 out=words[:].rearrange("p r q -> p (r q)").bitcast(FP8X4),
                 scales=scales[:].rearrange("p r q -> p (r q)"),
-                in_=grouped[:].rearrange("p r q j -> p (r q j)"),
+                in_=grouped_of[t][:].rearrange("p r q j -> p (r q j)"),
             )
+            packed_of[t] = (words, scales)
 
-            if t % PHI_STEPS == 0:
-                phi_st = [
-                    stage.tile([P, PHI_STEPS * STEP], F32, name="phi_st%d" % m) for m in range(D_TILES)
-                ]
+        def multiply_and_store(t):
+            words, scales = packed_of[t]
             first = (t % PHI_STEPS) * STEP
             for m in range(D_TILES):
+                if first == 0:
+                    phi_st[m] = stage.tile([P, PHI_STEPS * STEP], F32, name="phi_st%d" % m)
                 phi_ps = psum.tile([P, STEP], F32, tag="phi_ps")
                 nc.tensor.matmul_mx(
                     out=phi_ps[:],
@@ -208,7 +215,7 @@ def tile_nlgate_pa_t_kernel(tc, v, a, Wp_words, Wp_scales, bp, Wg_words, Wg_scal
                     bias=phi_bias[:, m, t : t + 1],
                     scale=1.0,
                 )
-                if t % PHI_STEPS == PHI_STEPS - 1:
+                if first == (PHI_STEPS - 1) * STEP:
                     last = (t + 1) * STEP
                     nc.sync.dma_start(out=phi_rows[m, :, last - PHI_STEPS * STEP : last], in_=phi_st[m][:])
 
@@ -241,3 +248,13 @@ def tile_nlgate_pa_t_kernel(tc, v, a, Wp_words, Wp_scales, bp, Wg_words, Wg_scal
                     op=ADD,
                 )
             nc.sync.dma_start(out=g_rows[t], in_=g_st[:].rearrange("q r d -> q (r d)"))
+
+        regroup(0)
+        regroup(1)
+        quantise(0)
+        for t in range(T):
+            if t + 2 < T:
+                regroup(t + 2)
+            if t + 1 < T:
+                quantise(t + 1)
+            multiply_and_store(t)

@@ -22,7 +22,8 @@ D_TILES = D // P
 STEP = N // T
 ROWS = STEP // P
 A_CHUNK = 2048
-PHI_STEPS = 2
+PHI_STEPS = 4
+G_STEPS = 2
 Z_REP = 4
 T_VECTOR = 10
 T_SCALAR = T - T_VECTOR
@@ -51,11 +52,12 @@ def tile_nlgate_pa_t_kernel(tc, v, a, Wp_words, Wp_scales, bp, Wg_words, Wg_scal
     v_rows = v[0].rearrange("(p j) t h w -> p j (t h w)", j=PACK)
     a_rows = a[0].rearrange("(p j) i f -> p j (i f)", j=PACK)
     phi_rows = out_0[0].rearrange("(m d) n -> m d n", d=P)
-    g_rows = out_1[0].rearrange("(t q r) d -> t q (r d)", q=P, r=ROWS)
+    g_rows = out_1[0].rearrange("(s u q r) d -> s q u (r d)", u=G_STEPS, q=P, r=ROWS)
 
     with ExitStack() as ctx:
         keep = ctx.enter_context(tc.tile_pool(name="keep", bufs=1))
         stage = ctx.enter_context(tc.tile_pool(name="stage", bufs=4))
+        outs = ctx.enter_context(tc.tile_pool(name="outs", bufs=3))
         psum = ctx.enter_context(tc.psum_pool(name="psum", bufs=4))
         ctx.enter_context(tc.manual_schedule())
 
@@ -171,6 +173,7 @@ def tile_nlgate_pa_t_kernel(tc, v, a, Wp_words, Wp_scales, bp, Wg_words, Wg_scal
 
         grouped_of = {}
         packed_of = {}
+        g_st_of = {}
         phi_st = {}
 
         def regroup(t):
@@ -197,7 +200,7 @@ def tile_nlgate_pa_t_kernel(tc, v, a, Wp_words, Wp_scales, bp, Wg_words, Wg_scal
             first = (t % PHI_STEPS) * STEP
             for m in range(D_TILES):
                 if first == 0:
-                    phi_st[m] = stage.tile([P, PHI_STEPS * STEP], F32, name="phi_st%d" % m)
+                    phi_st[m] = outs.tile([P, PHI_STEPS * STEP], F32, name="phi_st%d" % m)
                 phi_ps = psum.tile([P, STEP], F32, tag="phi_ps")
                 nc.tensor.matmul_mx(
                     out=phi_ps[:],
@@ -219,7 +222,10 @@ def tile_nlgate_pa_t_kernel(tc, v, a, Wp_words, Wp_scales, bp, Wg_words, Wg_scal
                     last = (t + 1) * STEP
                     nc.sync.dma_start(out=phi_rows[m, :, last - PHI_STEPS * STEP : last], in_=phi_st[m][:])
 
-            g_st = stage.tile([P, ROWS, D], F32)
+            u = t % G_STEPS
+            if u == 0:
+                g_st_of[0] = outs.tile([P, G_STEPS, ROWS, D], F32, name="g_st")
+            g_st = g_st_of[0]
             for r0 in range(0, ROWS, 2):
                 g_ps = psum.tile([P, 2, D], F32, tag="g_ps")
                 for i in range(2):
@@ -242,12 +248,13 @@ def tile_nlgate_pa_t_kernel(tc, v, a, Wp_words, Wp_scales, bp, Wg_words, Wg_scal
                         stop=True,
                     )
                 nc.vector.tensor_tensor(
-                    out=g_st[:, r0 : r0 + 2, :],
+                    out=g_st[:, u, r0 : r0 + 2, :],
                     in0=g_ps[:],
                     in1=bg_sb[:].unsqueeze(1).to_broadcast([P, 2, D]),
                     op=ADD,
                 )
-            nc.sync.dma_start(out=g_rows[t], in_=g_st[:].rearrange("q r d -> q (r d)"))
+            if u == G_STEPS - 1:
+                nc.sync.dma_start(out=g_rows[t // G_STEPS], in_=g_st[:].rearrange("q u r d -> q u (r d)"))
 
         regroup(0)
         regroup(1)

@@ -1,6 +1,7 @@
 from contextlib import ExitStack
 
 import concourse.mybir as mybir
+from concourse.masks import make_identity
 
 BF16 = mybir.dt.bfloat16
 F32 = mybir.dt.float32
@@ -25,8 +26,8 @@ A_CHUNK = 2048
 PHI_STEPS = 4
 G_STEPS = 2
 Z_REP = 4
-T_VECTOR = 10
-T_SCALAR = T - T_VECTOR
+HW_RUN = 28
+HW_PARTS = HW // HW_RUN
 
 FLOPS = 2 * 2 * D * (2 * P * PACK) * N
 
@@ -61,6 +62,11 @@ def tile_nlgate_pa_t_kernel(tc, v, a, Wp_words, Wp_scales, bp, Wg_words, Wg_scal
         psum = ctx.enter_context(tc.psum_pool(name="psum", bufs=4))
         ctx.enter_context(tc.manual_schedule())
 
+        bias_rows = keep.tile([P, 2 * D], BF16)
+        nc.vector.memset(bias_rows[:], 0.0)
+        nc.scalar.dma_start(out=bias_rows[0:1, 0:D], in_=bp.rearrange("(o d) -> o d", o=1))
+        nc.scalar.dma_start(out=bias_rows[0:1, D : 2 * D], in_=bg.rearrange("(o d) -> o d", o=1))
+
         v_sb = []
         for j in range(PACK):
             v_j = keep.tile([P, T * HW], BF16, name="v%d" % j)
@@ -74,12 +80,13 @@ def tile_nlgate_pa_t_kernel(tc, v, a, Wp_words, Wp_scales, bp, Wg_words, Wg_scal
             nc.sync.dma_start(out=a_c[:], in_=a_rows[:, :, c * A_CHUNK : (c + 1) * A_CHUNK])
             a_sb.append(a_c)
 
-        bias_rows = keep.tile([P, 2 * D], BF16)
-        nc.vector.memset(bias_rows[:], 0.0)
-        nc.scalar.dma_start(out=bias_rows[0:1, 0:D], in_=bp.rearrange("(o d) -> o d", o=1))
-        nc.scalar.dma_start(out=bias_rows[0:1, D : 2 * D], in_=bg.rearrange("(o d) -> o d", o=1))
         ones = keep.tile([P, P], BF16)
         nc.vector.memset(ones[:], 1.0)
+        identity = keep.tile([P, P], BF16)
+        make_identity(nc, identity[:])
+        warm = keep.tile([P, 1], F32)
+        nc.scalar.activation(out=warm[:], in_=ones[:, 0:1], func=ACT.Identity)
+
         bias_ps = psum.tile([P, STEP], F32, tag="phi_ps")
         nc.tensor.matmul(out=bias_ps[:, 0:D], lhsT=ones[:], rhs=bias_rows[:, D : 2 * D], start=True, stop=True)
         for m in range(D_TILES):
@@ -97,34 +104,19 @@ def tile_nlgate_pa_t_kernel(tc, v, a, Wp_words, Wp_scales, bp, Wg_words, Wg_scal
             out=bp_sb[:], in_=bias_ps[:, D : D + 32 * D_TILES].rearrange("p (m x) -> p m x", x=32)[:, :, 0]
         )
 
-        sums_vector = keep.tile([P, PACK, T_VECTOR], F32)
-        sums_scalar = keep.tile([P, PACK, T_SCALAR], F32)
+        sums = keep.tile([P, PACK, T], F32)
         for j in range(PACK):
-            nc.vector.tensor_reduce(
-                out=sums_vector[:, j, :],
-                in_=v_sb[j][:, 0 : T_VECTOR * HW].rearrange("p (t s) -> p t s", s=HW),
-                axis=mybir.AxisListType.X,
-                op=ADD,
-            )
-            for i in range(T_SCALAR):
-                unused = stage.tile([P, HW], BF16)
-                nc.scalar.activation(
-                    out=unused[:],
-                    in_=v_sb[j][:, (T_VECTOR + i) * HW : (T_VECTOR + i + 1) * HW],
-                    func=ACT.Copy,
-                    accum_out=sums_scalar[:, j, i : i + 1],
+            parts = v_sb[j][:].rearrange("p (t c s) -> p c t s", c=HW_PARTS, s=HW_RUN)
+            sum_ps = psum.tile([P, T, HW_RUN], F32, tag="phi_ps" if j < 2 else "g_ps")
+            for c in range(HW_PARTS):
+                nc.tensor.matmul(
+                    out=sum_ps[:], lhsT=identity[:], rhs=parts[:, c], start=(c == 0), stop=(c == HW_PARTS - 1)
                 )
+            nc.vector.tensor_reduce(out=sums[:, j, :], in_=sum_ps[:], axis=mybir.AxisListType.X, op=ADD)
         z_grouped = keep.tile([P, T, Z_REP, PACK], BF16, align_bytes=64)
         nc.vector.tensor_scalar(
-            out=z_grouped[:, 0:T_VECTOR, :, :],
-            in0=sums_vector[:].rearrange("p j t -> p t j").unsqueeze(2).to_broadcast([P, T_VECTOR, Z_REP, PACK]),
-            scalar1=1.0 / HW,
-            scalar2=None,
-            op0=MULT,
-        )
-        nc.vector.tensor_scalar(
-            out=z_grouped[:, T_VECTOR:T, :, :],
-            in0=sums_scalar[:].rearrange("p j t -> p t j").unsqueeze(2).to_broadcast([P, T_SCALAR, Z_REP, PACK]),
+            out=z_grouped[:],
+            in0=sums[:].rearrange("p j t -> p t j").unsqueeze(2).to_broadcast([P, T, Z_REP, PACK]),
             scalar1=1.0 / HW,
             scalar2=None,
             op0=MULT,

@@ -23,8 +23,9 @@ D_TILES = D // P
 STEP = N // T
 ROWS = STEP // P
 A_CHUNK = 2048
-PHI_STEPS = 4
-G_STEPS = 2
+DOUBLE = 2 * STEP
+UNITS = N // STEP
+PHI_DOUBLES = 2
 Z_REP = 4
 HW_RUN = 28
 HW_PARTS = HW // HW_RUN
@@ -53,7 +54,7 @@ def tile_nlgate_pa_t_kernel(tc, v, a, Wp_words, Wp_scales, bp, Wg_words, Wg_scal
     v_rows = v[0].rearrange("(p j) t h w -> p j (t h w)", j=PACK)
     a_rows = a[0].rearrange("(p j) i f -> p j (i f)", j=PACK)
     phi_rows = out_0[0].rearrange("(m d) n -> m d n", d=P)
-    g_rows = out_1[0].rearrange("(s u q r) d -> s q u (r d)", u=G_STEPS, q=P, r=ROWS)
+    g_rows = out_1[0].rearrange("(s q r) d -> s q (r d)", q=P, r=2 * ROWS)
 
     with ExitStack() as ctx:
         keep = ctx.enter_context(tc.tile_pool(name="keep", bufs=1))
@@ -142,15 +143,15 @@ def tile_nlgate_pa_t_kernel(tc, v, a, Wp_words, Wp_scales, bp, Wg_words, Wg_scal
                 stop=True,
             )
 
-        zz_words = keep.tile([P, T, P], U32, align_bytes=64)
+        zz_words = keep.tile([P, T, P // 2], U32, align_bytes=64)
         nc.vector.tensor_copy(
             out=zz_words[:].bitcast(I32),
-            in_=z_words[:].bitcast(I32).rearrange("p (t x) -> p t x", x=Z_REP)[:, :, 0:1].to_broadcast([P, T, P]),
+            in_=z_words[:].bitcast(I32).rearrange("p (t x) -> p t x", x=Z_REP)[:, :, 0:1].to_broadcast([P, T, P // 2]),
         )
-        zz_scales = keep.tile([P, T, P], U8, align_bytes=64)
+        zz_scales = keep.tile([P, T, P // 2], U8, align_bytes=64)
         nc.vector.tensor_copy(
             out=zz_scales[:].bitcast(I32),
-            in_=z_scales[:].bitcast(I32).unsqueeze(2).to_broadcast([P, T, P // 4]),
+            in_=z_scales[:].bitcast(I32).unsqueeze(2).to_broadcast([P, T, P // 8]),
         )
 
         phi_bias = keep.tile([P, D_TILES, T], F32)
@@ -168,31 +169,33 @@ def tile_nlgate_pa_t_kernel(tc, v, a, Wp_words, Wp_scales, bp, Wg_words, Wg_scal
         g_st_of = {}
         phi_st = {}
 
-        def regroup(t):
-            c, u = divmod(t, A_CHUNK // STEP)
-            columns = a_sb[c][:, :, u * STEP : (u + 1) * STEP].rearrange("p j (q r) -> p q j r", r=ROWS)
+        def regroup(e):
+            s, h = divmod(e, 2)
+            c, u = divmod(s, A_CHUNK // DOUBLE)
+            columns = a_sb[c][:, :, u * DOUBLE : (u + 1) * DOUBLE].rearrange("p j (q h r) -> p h q j r", h=2, r=ROWS)
             grouped = stage.tile([P, ROWS, P, PACK], BF16, align_bytes=64)
             regions = grouped[:].rearrange("p r q j -> p q j r")
-            nc.vector.tensor_copy(out=regions[:, 0 : P // 2], in_=columns[:, 0 : P // 2])
-            nc.scalar.copy(out=regions[:, P // 2 : P], in_=columns[:, P // 2 : P])
-            grouped_of[t] = grouped
+            nc.vector.tensor_copy(out=regions[:, 0 : P // 2], in_=columns[:, h, 0 : P // 2])
+            nc.scalar.copy(out=regions[:, P // 2 : P], in_=columns[:, h, P // 2 : P])
+            grouped_of[e] = grouped
 
-        def quantise(t):
+        def quantise(e):
             words = stage.tile([P, ROWS, P], U32, align_bytes=64)
             scales = stage.tile([P, ROWS, P], U8, align_bytes=64)
             nc.vector.quantize_mx(
                 out=words[:].rearrange("p r q -> p (r q)").bitcast(FP8X4),
                 scales=scales[:].rearrange("p r q -> p (r q)"),
-                in_=grouped_of[t][:].rearrange("p r q j -> p (r q j)"),
+                in_=grouped_of[e][:].rearrange("p r q j -> p (r q j)"),
             )
-            packed_of[t] = (words, scales)
+            packed_of[e] = (words, scales)
 
-        def multiply_and_store(t):
-            words, scales = packed_of[t]
-            first = (t % PHI_STEPS) * STEP
+        def multiply_and_store(e):
+            s, h = divmod(e, 2)
+            words, scales = packed_of[e]
+            first = (s % PHI_DOUBLES) * DOUBLE
             for m in range(D_TILES):
-                if first == 0:
-                    phi_st[m] = outs.tile([P, PHI_STEPS * STEP], F32, name="phi_st%d" % m)
+                if first == 0 and h == 0:
+                    phi_st[m] = outs.tile([P, PHI_DOUBLES * DOUBLE], F32, name="phi_st%d" % m)
                 phi_ps = psum.tile([P, STEP], F32, tag="phi_ps")
                 nc.tensor.matmul_mx(
                     out=phi_ps[:],
@@ -203,20 +206,22 @@ def tile_nlgate_pa_t_kernel(tc, v, a, Wp_words, Wp_scales, bp, Wg_words, Wg_scal
                     start=True,
                     stop=True,
                 )
-                nc.scalar.activation(
-                    out=phi_st[m][:, first : first + STEP].rearrange("d (q r) -> d q r", r=ROWS),
-                    in_=phi_ps[:].rearrange("d (r q) -> d q r", r=ROWS),
-                    func=ACT.Identity,
-                    bias=phi_bias[:, m, t : t + 1],
-                    scale=1.0,
-                )
-                if first == (PHI_STEPS - 1) * STEP:
-                    last = (t + 1) * STEP
-                    nc.sync.dma_start(out=phi_rows[m, :, last - PHI_STEPS * STEP : last], in_=phi_st[m][:])
+                target = phi_st[m][:, first : first + DOUBLE].rearrange("d (q h r) -> d h q r", h=2, r=ROWS)
+                source = phi_ps[:].rearrange("d (r q) -> d q r", r=ROWS)
+                for w in range(2):
+                    nc.scalar.activation(
+                        out=target[:, h, (P // 2) * w : (P // 2) * (w + 1), :],
+                        in_=source[:, (P // 2) * w : (P // 2) * (w + 1), :],
+                        func=ACT.Identity,
+                        bias=phi_bias[:, m, 2 * s + w : 2 * s + w + 1],
+                        scale=1.0,
+                    )
+                if first == (PHI_DOUBLES - 1) * DOUBLE and h == 1:
+                    last = (s + 1) * DOUBLE
+                    nc.sync.dma_start(out=phi_rows[m, :, last - PHI_DOUBLES * DOUBLE : last], in_=phi_st[m][:])
 
-            u = t % G_STEPS
-            if u == 0:
-                g_st_of[0] = outs.tile([P, G_STEPS, ROWS, D], F32, name="g_st")
+            if h == 0:
+                g_st_of[0] = outs.tile([P, 2 * ROWS, D], F32, name="g_st")
             g_st = g_st_of[0]
             for r0 in range(0, ROWS, 2):
                 g_ps = psum.tile([P, 2, D], F32, tag="g_ps")
@@ -232,28 +237,28 @@ def tile_nlgate_pa_t_kernel(tc, v, a, Wp_words, Wp_scales, bp, Wg_words, Wg_scal
                     )
                     nc.tensor.matmul_mx(
                         out=g_ps[:, i, :],
-                        lhsT=zz_words[:, t, :].bitcast(FP8X4),
-                        lhsT_scale=zz_scales[:, t, :],
+                        lhsT=zz_words[:, 2 * s : 2 * s + 2, :].rearrange("p t q -> p (t q)").bitcast(FP8X4),
+                        lhsT_scale=zz_scales[:, 2 * s : 2 * s + 2, :].rearrange("p t q -> p (t q)"),
                         rhs=wg_words[:, 1, :].bitcast(FP8X4),
                         rhs_scale=wg_scales[:, 1, :],
                         start=False,
                         stop=True,
                     )
                 nc.vector.tensor_tensor(
-                    out=g_st[:, u, r0 : r0 + 2, :],
+                    out=g_st[:, ROWS * h + r0 : ROWS * h + r0 + 2, :],
                     in0=g_ps[:],
                     in1=bg_sb[:].unsqueeze(1).to_broadcast([P, 2, D]),
                     op=ADD,
                 )
-            if u == G_STEPS - 1:
-                nc.sync.dma_start(out=g_rows[t // G_STEPS], in_=g_st[:].rearrange("q u r d -> q u (r d)"))
+            if h == 1:
+                nc.sync.dma_start(out=g_rows[s], in_=g_st[:].rearrange("q r d -> q (r d)"))
 
         regroup(0)
         regroup(1)
         quantise(0)
-        for t in range(T):
-            if t + 2 < T:
-                regroup(t + 2)
-            if t + 1 < T:
-                quantise(t + 1)
-            multiply_and_store(t)
+        for e in range(UNITS):
+            if e + 2 < UNITS:
+                regroup(e + 2)
+            if e + 1 < UNITS:
+                quantise(e + 1)
+            multiply_and_store(e)

@@ -22,10 +22,10 @@ D = 256
 D_TILES = D // P
 STEP = N // T
 ROWS = STEP // P
-A_CHUNK = 2048
+A_WIDTHS = (1024, 1024, 2048, 4096)
 DOUBLE = 2 * STEP
 UNITS = N // STEP
-PHI_DOUBLES = 2
+PHI_GROUPS = (2, 2, 2, 1, 1)
 Z_REP = 4
 HW_RUN = 28
 HW_PARTS = HW // HW_RUN
@@ -55,6 +55,7 @@ def tile_nlgate_pa_t_kernel(tc, v, a, Wp_words, Wp_scales, bp, Wg_words, Wg_scal
     a_rows = a[0].rearrange("(p j) i f -> p j (i f)", j=PACK)
     phi_rows = out_0[0].rearrange("(m d) n -> m d n", d=P)
     g_rows = out_1[0].rearrange("(s q r) d -> s q (r d)", q=P, r=2 * ROWS)
+    g_halves = out_1[0].rearrange("(s q h r) d -> s h q (r d)", q=P, h=2, r=ROWS)
 
     with ExitStack() as ctx:
         keep = ctx.enter_context(tc.tile_pool(name="keep", bufs=1))
@@ -75,11 +76,14 @@ def tile_nlgate_pa_t_kernel(tc, v, a, Wp_words, Wp_scales, bp, Wg_words, Wg_scal
             v_sb.append(v_j)
         wp_words, wp_scales = load_weight(nc, keep, Wp_words, Wp_scales, "wp")
         wg_words, wg_scales = load_weight(nc, keep, Wg_words, Wg_scales, "wg")
-        a_sb = []
-        for c in range(N // A_CHUNK):
-            a_c = keep.tile([P, PACK, A_CHUNK], BF16, name="a%d" % c)
-            nc.sync.dma_start(out=a_c[:], in_=a_rows[:, :, c * A_CHUNK : (c + 1) * A_CHUNK])
-            a_sb.append(a_c)
+        a_of = {}
+        a_first = 0
+        for c, width in enumerate(A_WIDTHS):
+            a_c = keep.tile([P, PACK, width], BF16, name="a%d" % c)
+            nc.sync.dma_start(out=a_c[:], in_=a_rows[:, :, a_first : a_first + width])
+            for u in range(width // DOUBLE):
+                a_of[a_first // DOUBLE + u] = (a_c, u * DOUBLE)
+            a_first += width
 
         ones = keep.tile([P, P], BF16)
         nc.vector.memset(ones[:], 1.0)
@@ -168,11 +172,17 @@ def tile_nlgate_pa_t_kernel(tc, v, a, Wp_words, Wp_scales, bp, Wg_words, Wg_scal
         packed_of = {}
         g_st_of = {}
         phi_st = {}
+        group_of = {}
+        group_first = 0
+        for size in PHI_GROUPS:
+            for s in range(group_first, group_first + size):
+                group_of[s] = (group_first, size)
+            group_first += size
 
         def regroup(e):
             s, h = divmod(e, 2)
-            c, u = divmod(s, A_CHUNK // DOUBLE)
-            columns = a_sb[c][:, :, u * DOUBLE : (u + 1) * DOUBLE].rearrange("p j (q h r) -> p h q j r", h=2, r=ROWS)
+            a_c, begin = a_of[s]
+            columns = a_c[:, :, begin : begin + DOUBLE].rearrange("p j (q h r) -> p h q j r", h=2, r=ROWS)
             grouped = stage.tile([P, ROWS, P, PACK], BF16, align_bytes=64)
             regions = grouped[:].rearrange("p r q j -> p q j r")
             nc.vector.tensor_copy(out=regions[:, 0 : P // 2], in_=columns[:, h, 0 : P // 2])
@@ -192,10 +202,11 @@ def tile_nlgate_pa_t_kernel(tc, v, a, Wp_words, Wp_scales, bp, Wg_words, Wg_scal
         def multiply_and_store(e):
             s, h = divmod(e, 2)
             words, scales = packed_of[e]
-            first = (s % PHI_DOUBLES) * DOUBLE
+            group_s, size = group_of[s]
+            first = (s - group_s) * DOUBLE
             for m in range(D_TILES):
                 if first == 0 and h == 0:
-                    phi_st[m] = outs.tile([P, PHI_DOUBLES * DOUBLE], F32, name="phi_st%d" % m)
+                    phi_st[m] = outs.tile([P, size * DOUBLE], F32, name="phi_st%d" % m)
                 phi_ps = psum.tile([P, STEP], F32, tag="phi_ps")
                 nc.tensor.matmul_mx(
                     out=phi_ps[:],
@@ -216,9 +227,8 @@ def tile_nlgate_pa_t_kernel(tc, v, a, Wp_words, Wp_scales, bp, Wg_words, Wg_scal
                         bias=phi_bias[:, m, 2 * s + w : 2 * s + w + 1],
                         scale=1.0,
                     )
-                if first == (PHI_DOUBLES - 1) * DOUBLE and h == 1:
-                    last = (s + 1) * DOUBLE
-                    nc.sync.dma_start(out=phi_rows[m, :, last - PHI_DOUBLES * DOUBLE : last], in_=phi_st[m][:])
+                if first == (size - 1) * DOUBLE and h == 1:
+                    nc.sync.dma_start(out=phi_rows[m, :, group_s * DOUBLE : (s + 1) * DOUBLE], in_=phi_st[m][:])
 
             if h == 0:
                 g_st_of[0] = outs.tile([P, 2 * ROWS, D], F32, name="g_st")
@@ -250,7 +260,11 @@ def tile_nlgate_pa_t_kernel(tc, v, a, Wp_words, Wp_scales, bp, Wg_words, Wg_scal
                     in1=bg_sb[:].unsqueeze(1).to_broadcast([P, 2, D]),
                     op=ADD,
                 )
-            if h == 1:
+            if s == UNITS // 2 - 1:
+                nc.sync.dma_start(
+                    out=g_halves[s, h], in_=g_st[:, ROWS * h : ROWS * (h + 1), :].rearrange("q r d -> q (r d)")
+                )
+            elif h == 1:
                 nc.sync.dma_start(out=g_rows[s], in_=g_st[:].rearrange("q r d -> q (r d)"))
 
         regroup(0)

@@ -33,12 +33,7 @@ HW_PARTS = HW // HW_RUN
 FLOPS = 2 * 2 * D * (2 * P * PACK) * N
 
 
-def load_weight(nc, pool, words, scales, label):
-    w_words = pool.tile([P, 2, D], U32, name=label + "_words", align_bytes=64)
-    nc.sync.dma_start(
-        out=w_words[:].bitcast(I32),
-        in_=words.rearrange("g p d j -> p g (d j)").bitcast(I32),
-    )
+def load_scales(nc, pool, scales, label):
     w_scales = pool.tile([P, 2, D], U8, name=label + "_scales", align_bytes=64)
     nc.vector.memset(w_scales[:].bitcast(I32), 0)
     for quadrant in range(4):
@@ -46,7 +41,16 @@ def load_weight(nc, pool, words, scales, label):
             out=w_scales[32 * quadrant : 32 * quadrant + 4, :, :].bitcast(I32),
             in_=scales[:, 4 * quadrant : 4 * quadrant + 4, :].rearrange("g b d -> b g d").bitcast(I32),
         )
-    return w_words, w_scales
+    return w_scales
+
+
+def load_words(nc, pool, words, label):
+    w_words = pool.tile([P, 2, D], U32, name=label + "_words", align_bytes=64)
+    nc.sync.dma_start(
+        out=w_words[:].bitcast(I32),
+        in_=words.rearrange("g p d j -> p g (d j)").bitcast(I32),
+    )
+    return w_words
 
 
 def tile_nlgate_pa_t_kernel(tc, v, a, Wp_words, Wp_scales, bp, Wg_words, Wg_scales, bg, out_0, out_1):
@@ -72,18 +76,36 @@ def tile_nlgate_pa_t_kernel(tc, v, a, Wp_words, Wp_scales, bp, Wg_words, Wg_scal
         v_sb = []
         for j in range(PACK):
             v_j = keep.tile([P, T * HW], BF16, name="v%d" % j)
-            nc.sync.dma_start(out=v_j[:], in_=v_rows[:, j, :])
             v_sb.append(v_j)
-        wp_words, wp_scales = load_weight(nc, keep, Wp_words, Wp_scales, "wp")
-        wg_words, wg_scales = load_weight(nc, keep, Wg_words, Wg_scales, "wg")
+        a_sb = []
         a_of = {}
         a_first = 0
         for c, width in enumerate(A_WIDTHS):
             a_c = keep.tile([P, PACK, width], BF16, name="a%d" % c)
-            nc.sync.dma_start(out=a_c[:], in_=a_rows[:, :, a_first : a_first + width])
+            a_sb.append((a_c, a_first, width))
             for u in range(width // DOUBLE):
                 a_of[a_first // DOUBLE + u] = (a_c, u * DOUBLE)
             a_first += width
+
+        def load_v(j):
+            nc.sync.dma_start(out=v_sb[j][:], in_=v_rows[:, j, :])
+
+        def load_a(c):
+            a_c, begin, width = a_sb[c]
+            nc.sync.dma_start(out=a_c[:], in_=a_rows[:, :, begin : begin + width])
+
+        load_v(0)
+        load_v(1)
+        wp_scales = load_scales(nc, keep, Wp_scales, "wp")
+        load_v(2)
+        load_v(3)
+        wp_words = load_words(nc, keep, Wp_words, "wp")
+        wg_words = load_words(nc, keep, Wg_words, "wg")
+        load_a(0)
+        wg_scales = load_scales(nc, keep, Wg_scales, "wg")
+        load_a(1)
+        load_a(2)
+        load_a(3)
 
         ones = keep.tile([P, P], BF16)
         nc.vector.memset(ones[:], 1.0)

@@ -22,7 +22,7 @@ D = 256
 D_TILES = D // P
 STEP = N // T
 ROWS = STEP // P
-A_WIDTHS = (1024, 1024, 2048, 4096)
+A_WIDTHS = (2048, 2048, 4096)
 DOUBLE = 2 * STEP
 UNITS = N // STEP
 PHI_GROUPS = (2, 2, 2, 1, 1)
@@ -74,9 +74,9 @@ def tile_nlgate_pa_t_kernel(tc, v, a, Wp_words, Wp_scales, bp, Wg_words, Wg_scal
         nc.scalar.dma_start(out=bias_rows[0:1, D : 2 * D], in_=bg.rearrange("(o d) -> o d", o=1))
 
         v_sb = []
-        for j in range(PACK):
-            v_j = keep.tile([P, T * HW], BF16, name="v%d" % j)
-            v_sb.append(v_j)
+        for i in range(PACK // 2):
+            v_i = keep.tile([P, 2, T * HW], BF16, name="v%d" % i)
+            v_sb.append(v_i)
         a_sb = []
         a_of = {}
         a_first = 0
@@ -87,25 +87,22 @@ def tile_nlgate_pa_t_kernel(tc, v, a, Wp_words, Wp_scales, bp, Wg_words, Wg_scal
                 a_of[a_first // DOUBLE + u] = (a_c, u * DOUBLE)
             a_first += width
 
-        def load_v(j):
-            nc.sync.dma_start(out=v_sb[j][:], in_=v_rows[:, j, :])
+        def load_v(i):
+            nc.sync.dma_start(out=v_sb[i][:], in_=v_rows[:, 2 * i : 2 * i + 2, :])
 
         def load_a(c):
             a_c, begin, width = a_sb[c]
             nc.sync.dma_start(out=a_c[:], in_=a_rows[:, :, begin : begin + width])
 
         load_v(0)
-        load_v(1)
         wp_scales = load_scales(nc, keep, Wp_scales, "wp")
-        load_v(2)
-        load_v(3)
+        load_v(1)
         wp_words = load_words(nc, keep, Wp_words, "wp")
         wg_words = load_words(nc, keep, Wg_words, "wg")
         load_a(0)
         wg_scales = load_scales(nc, keep, Wg_scales, "wg")
         load_a(1)
         load_a(2)
-        load_a(3)
 
         ones = keep.tile([P, P], BF16)
         nc.vector.memset(ones[:], 1.0)
@@ -133,7 +130,7 @@ def tile_nlgate_pa_t_kernel(tc, v, a, Wp_words, Wp_scales, bp, Wg_words, Wg_scal
 
         sums = keep.tile([P, PACK, T], F32)
         for j in range(PACK):
-            parts = v_sb[j][:].rearrange("p (t c s) -> p c t s", c=HW_PARTS, s=HW_RUN)
+            parts = v_sb[j // 2][:, j % 2, :].rearrange("p (t c s) -> p c t s", c=HW_PARTS, s=HW_RUN)
             sum_ps = psum.tile([P, T, HW_RUN], F32, tag="phi_ps" if j < 2 else "g_ps")
             for c in range(HW_PARTS):
                 nc.tensor.matmul(

@@ -70,9 +70,6 @@ def tile_nlgate_pa_t_kernel(tc, v, a, Wp_words, Wp_scales, bp, Wg_words, Wg_scal
 
         bias_rows = keep.tile([P, 2 * D], BF16)
         nc.vector.memset(bias_rows[:], 0.0)
-        nc.scalar.dma_start(out=bias_rows[0:1, 0:D], in_=bp.rearrange("(o d) -> o d", o=1))
-        nc.scalar.dma_start(out=bias_rows[0:1, D : 2 * D], in_=bg.rearrange("(o d) -> o d", o=1))
-
         v_sb = []
         for i in range(PACK // 2):
             v_i = keep.tile([P, 2, T * HW], BF16, name="v%d" % i)
@@ -96,6 +93,8 @@ def tile_nlgate_pa_t_kernel(tc, v, a, Wp_words, Wp_scales, bp, Wg_words, Wg_scal
 
         load_v(0)
         wp_scales = load_scales(nc, keep, Wp_scales, "wp")
+        nc.sync.dma_start(out=bias_rows[0:1, 0:D], in_=bp.rearrange("(o d) -> o d", o=1))
+        nc.sync.dma_start(out=bias_rows[0:1, D : 2 * D], in_=bg.rearrange("(o d) -> o d", o=1))
         load_v(1)
         wp_words = load_words(nc, keep, Wp_words, "wp")
         wg_words = load_words(nc, keep, Wg_words, "wg")
@@ -110,23 +109,6 @@ def tile_nlgate_pa_t_kernel(tc, v, a, Wp_words, Wp_scales, bp, Wg_words, Wg_scal
         make_identity(nc, identity[:])
         warm = keep.tile([P, 1], F32)
         nc.scalar.activation(out=warm[:], in_=ones[:, 0:1], func=ACT.Identity)
-
-        bias_ps = psum.tile([P, STEP], F32, tag="phi_ps")
-        nc.tensor.matmul(out=bias_ps[:, 0:D], lhsT=ones[:], rhs=bias_rows[:, D : 2 * D], start=True, stop=True)
-        for m in range(D_TILES):
-            nc.tensor.matmul(
-                out=bias_ps[:, D + 32 * m : D + 32 * (m + 1)],
-                lhsT=bias_rows[:, P * m : P * (m + 1)],
-                rhs=ones[:, 0:32],
-                start=True,
-                stop=True,
-            )
-        bg_sb = keep.tile([P, D], F32)
-        nc.vector.tensor_copy(out=bg_sb[:], in_=bias_ps[:, 0:D])
-        bp_sb = keep.tile([P, D_TILES], F32)
-        nc.vector.tensor_copy(
-            out=bp_sb[:], in_=bias_ps[:, D : D + 32 * D_TILES].rearrange("p (m x) -> p m x", x=32)[:, :, 0]
-        )
 
         sums = keep.tile([P, PACK, T], F32)
         for j in range(PACK):
@@ -152,6 +134,23 @@ def tile_nlgate_pa_t_kernel(tc, v, a, Wp_words, Wp_scales, bp, Wg_words, Wg_scal
             out=z_words[:].bitcast(FP8X4),
             scales=z_scales[:],
             in_=z_grouped[:].rearrange("p t x j -> p (t x j)"),
+        )
+
+        bias_ps = psum.tile([P, STEP], F32, tag="phi_ps")
+        nc.tensor.matmul(out=bias_ps[:, 0:D], lhsT=ones[:], rhs=bias_rows[:, D : 2 * D], start=True, stop=True)
+        for m in range(D_TILES):
+            nc.tensor.matmul(
+                out=bias_ps[:, D + 32 * m : D + 32 * (m + 1)],
+                lhsT=bias_rows[:, P * m : P * (m + 1)],
+                rhs=ones[:, 0:32],
+                start=True,
+                stop=True,
+            )
+        bg_sb = keep.tile([P, D], F32)
+        nc.vector.tensor_copy(out=bg_sb[:], in_=bias_ps[:, 0:D])
+        bp_sb = keep.tile([P, D_TILES], F32)
+        nc.vector.tensor_copy(
+            out=bp_sb[:], in_=bias_ps[:, D : D + 32 * D_TILES].rearrange("p (m x) -> p m x", x=32)[:, :, 0]
         )
 
         z_ps = psum.tile([P, D_TILES, D], F32, tag="g_ps")

@@ -45,7 +45,7 @@ def load_scales(nc, pool, scales, label):
 
 
 def load_words(nc, pool, words, label):
-    w_words = pool.tile([P, 2, D], U32, name=label + "_words", align_bytes=64)
+    w_words = pool.tile([P, 2, D], U32, name=label + "_words", align_bytes=256)
     nc.sync.dma_start(
         out=w_words[:].bitcast(I32),
         in_=words.rearrange("g p d j -> p g (d j)").bitcast(I32),
@@ -57,7 +57,7 @@ def tile_nlgate_pa_t_kernel(tc, v, a, Wp_words, Wp_scales, bp, Wg_words, Wg_scal
     nc = tc.nc
     v_rows = v[0].rearrange("(p j) t h w -> p j (t h w)", j=PACK)
     a_rows = a[0].rearrange("(p j) i f -> p j (i f)", j=PACK)
-    phi_rows = out_0[0].rearrange("(m d) n -> m d n", d=P)
+    phi_rows = out_0[0].rearrange("(m d) n -> d m n", d=P)
     g_rows = out_1[0].rearrange("(s q r) d -> s q (r d)", q=P, r=2 * ROWS)
     g_halves = out_1[0].rearrange("(s q h r) d -> s h q (r d)", q=P, h=2, r=ROWS)
 
@@ -72,13 +72,13 @@ def tile_nlgate_pa_t_kernel(tc, v, a, Wp_words, Wp_scales, bp, Wg_words, Wg_scal
         nc.vector.memset(bias_rows[:], 0.0)
         v_sb = []
         for i in range(PACK // 2):
-            v_i = keep.tile([P, 2, T * HW], BF16, name="v%d" % i)
+            v_i = keep.tile([P, 2, T * HW], BF16, name="v%d" % i, align_bytes=256)
             v_sb.append(v_i)
         a_sb = []
         a_of = {}
         a_first = 0
         for c, width in enumerate(A_WIDTHS):
-            a_c = keep.tile([P, PACK, width], BF16, name="a%d" % c)
+            a_c = keep.tile([P, PACK, width], BF16, name="a%d" % c, align_bytes=256)
             a_sb.append((a_c, a_first, width))
             for u in range(width // DOUBLE):
                 a_of[a_first // DOUBLE + u] = (a_c, u * DOUBLE)
@@ -189,7 +189,7 @@ def tile_nlgate_pa_t_kernel(tc, v, a, Wp_words, Wp_scales, bp, Wg_words, Wg_scal
         grouped_of = {}
         packed_of = {}
         g_st_of = {}
-        phi_st = {}
+        phi_st_of = {}
         group_of = {}
         group_first = 0
         for size in PHI_GROUPS:
@@ -223,8 +223,9 @@ def tile_nlgate_pa_t_kernel(tc, v, a, Wp_words, Wp_scales, bp, Wg_words, Wg_scal
             group_s, size = group_of[s]
             first = (s - group_s) * DOUBLE
             for m in range(D_TILES):
-                if first == 0 and h == 0:
-                    phi_st[m] = outs.tile([P, size * DOUBLE], F32, name="phi_st%d" % m)
+                if first == 0 and h == 0 and m == 0:
+                    phi_st_of[0] = outs.tile([P, D_TILES, size * DOUBLE], F32, name="phi_st", align_bytes=256)
+                phi_st = phi_st_of[0]
                 phi_ps = psum.tile([P, STEP], F32, tag="phi_ps")
                 nc.tensor.matmul_mx(
                     out=phi_ps[:],
@@ -235,7 +236,7 @@ def tile_nlgate_pa_t_kernel(tc, v, a, Wp_words, Wp_scales, bp, Wg_words, Wg_scal
                     start=True,
                     stop=True,
                 )
-                target = phi_st[m][:, first : first + DOUBLE].rearrange("d (q h r) -> d h q r", h=2, r=ROWS)
+                target = phi_st[:, m, first : first + DOUBLE].rearrange("d (q h r) -> d h q r", h=2, r=ROWS)
                 source = phi_ps[:].rearrange("d (r q) -> d q r", r=ROWS)
                 for w in range(2):
                     nc.scalar.activation(
@@ -245,11 +246,11 @@ def tile_nlgate_pa_t_kernel(tc, v, a, Wp_words, Wp_scales, bp, Wg_words, Wg_scal
                         bias=phi_bias[:, m, 2 * s + w : 2 * s + w + 1],
                         scale=1.0,
                     )
-                if first == (size - 1) * DOUBLE and h == 1:
-                    nc.sync.dma_start(out=phi_rows[m, :, group_s * DOUBLE : (s + 1) * DOUBLE], in_=phi_st[m][:])
+            if first == (size - 1) * DOUBLE and h == 1:
+                nc.sync.dma_start(out=phi_rows[:, :, group_s * DOUBLE : (s + 1) * DOUBLE], in_=phi_st_of[0][:])
 
             if h == 0:
-                g_st_of[0] = outs.tile([P, 2 * ROWS, D], F32, name="g_st")
+                g_st_of[0] = outs.tile([P, 2 * ROWS, D], F32, name="g_st", align_bytes=256)
             g_st = g_st_of[0]
             for r0 in range(0, ROWS, 2):
                 g_ps = psum.tile([P, 2, D], F32, tag="g_ps")

from contextlib import ExitStack

import concourse.mybir as mybir
from concourse.masks import make_identity

BF16 = mybir.dt.bfloat16
F32 = mybir.dt.float32
I32 = mybir.dt.int32
U32 = mybir.dt.uint32
U8 = mybir.dt.uint8
FP8X4 = mybir.dt.float8_e4m3fn_x4
ADD = mybir.AluOpType.add
MULT = mybir.AluOpType.mult
ACT = mybir.ActivationFunctionType

P = 128
PACK = 4
T = 16
HW = 14 * 14
N = 8192
D = 256
D_TILES = D // P
STEP = N // T
ROWS = STEP // P
A_WIDTHS = (2048, 2048, 4096)
DOUBLE = 2 * STEP
UNITS = N // STEP
PHI_GROUPS = (2, 2, 2, 1, 1)
Z_REP = 4
HW_RUN = 28
HW_PARTS = HW // HW_RUN

FLOPS = 2 * 2 * D * (2 * P * PACK) * N


def load_scales(nc, pool, scales, label):
    w_scales = pool.tile([P, 2, D], U8, name=label + "_scales", align_bytes=64)
    nc.vector.memset(w_scales[:].bitcast(I32), 0)
    for quadrant in range(4):
        nc.sync.dma_start(
            out=w_scales[32 * quadrant : 32 * quadrant + 4, :, :].bitcast(I32),
            in_=scales[:, 4 * quadrant : 4 * quadrant + 4, :].rearrange("g b d -> b g d").bitcast(I32),
        )
    return w_scales


def load_words(nc, pool, words, label):
    w_words = pool.tile([P, 2, D], U32, name=label + "_words", align_bytes=256)
    nc.sync.dma_start(
        out=w_words[:].bitcast(I32),
        in_=words.rearrange("g p d j -> p g (d j)").bitcast(I32),
    )
    return w_words


def tile_nlgate_pa_t_kernel(tc, v, a, Wp_words, Wp_scales, bp, Wg_words, Wg_scales, bg, out_0, out_1):
    nc = tc.nc
    v_rows = v[0].rearrange("(p j) t h w -> p j (t h w)", j=PACK)
    a_rows = a[0].rearrange("(p j) i f -> p j (i f)", j=PACK)
    phi_rows = out_0[0].rearrange("(m d) n -> d m n", d=P)
    g_rows = out_1[0].rearrange("(s q r) d -> s q (r d)", q=P, r=2 * ROWS)
    g_halves = out_1[0].rearrange("(s q h r) d -> s h q (r d)", q=P, h=2, r=ROWS)

    with ExitStack() as ctx:
        keep = ctx.enter_context(tc.tile_pool(name="keep", bufs=1))
        stage = ctx.enter_context(tc.tile_pool(name="stage", bufs=4))
        outs = ctx.enter_context(tc.tile_pool(name="outs", bufs=3))
        psum = ctx.enter_context(tc.psum_pool(name="psum", bufs=4))
        ctx.enter_context(tc.manual_schedule())

        bias_rows = keep.tile([P, 2 * D], BF16)
        nc.vector.memset(bias_rows[:], 0.0)
        v_sb = []
        for i in range(PACK // 2):
            v_i = keep.tile([P, 2, T * HW], BF16, name="v%d" % i, align_bytes=256)
            v_sb.append(v_i)
        a_sb = []
        a_of = {}
        a_first = 0
        for c, width in enumerate(A_WIDTHS):
            a_c = keep.tile([P, PACK, width], BF16, name="a%d" % c, align_bytes=256)
            a_sb.append((a_c, a_first, width))
            for u in range(width // DOUBLE):
                a_of[a_first // DOUBLE + u] = (a_c, u * DOUBLE)
            a_first += width

        def load_v(i):
            nc.sync.dma_start(out=v_sb[i][:], in_=v_rows[:, 2 * i : 2 * i + 2, :])

        def load_a(c):
            a_c, begin, width = a_sb[c]
            nc.sync.dma_start(out=a_c[:], in_=a_rows[:, :, begin : begin + width])

        load_v(0)
        wp_scales = load_scales(nc, keep, Wp_scales, "wp")
        nc.sync.dma_start(out=bias_rows[0:1, 0:D], in_=bp.rearrange("(o d) -> o d", o=1))
        nc.sync.dma_start(out=bias_rows[0:1, D : 2 * D], in_=bg.rearrange("(o d) -> o d", o=1))
        load_v(1)
        wp_words = load_words(nc, keep, Wp_words, "wp")
        wg_words = load_words(nc, keep, Wg_words, "wg")
        load_a(0)
        wg_scales = load_scales(nc, keep, Wg_scales, "wg")
        load_a(1)
        load_a(2)

        ones = keep.tile([P, P], BF16)
        nc.vector.memset(ones[:], 1.0)
        identity = keep.tile([P, P], BF16)
        make_identity(nc, identity[:])
        warm = keep.tile([P, 1], F32)
        nc.scalar.activation(out=warm[:], in_=ones[:, 0:1], func=ACT.Identity)

        sums = keep.tile([P, PACK, T], F32)
        for j in range(PACK):
            parts = v_sb[j // 2][:, j % 2, :].rearrange("p (t c s) -> p c t s", c=HW_PARTS, s=HW_RUN)
            sum_ps = psum.tile([P, T, HW_RUN], F32, tag="phi_ps" if j < 2 else "g_ps")
            for c in range(HW_PARTS):
                nc.tensor.matmul(
                    out=sum_ps[:], lhsT=identity[:], rhs=parts[:, c], start=(c == 0), stop=(c == HW_PARTS - 1)
                )
            nc.vector.tensor_reduce(out=sums[:, j, :], in_=sum_ps[:], axis=mybir.AxisListType.X, op=ADD)
        z_grouped = keep.tile([P, T, Z_REP, PACK], BF16, align_bytes=64)
        nc.vector.tensor_scalar(
            out=z_grouped[:],
            in0=sums[:].rearrange("p j t -> p t j").unsqueeze(2).to_broadcast([P, T, Z_REP, PACK]),
            scalar1=1.0 / HW,
            scalar2=None,
            op0=MULT,
        )
        z_words = keep.tile([P, T * Z_REP], U32, align_bytes=64)
        z_scales = keep.tile([P, T * Z_REP], U8, align_bytes=64)
        nc.vector.memset(z_scales[:].bitcast(I32), 0)
        nc.vector.quantize_mx(
            out=z_words[:].bitcast(FP8X4),
            scales=z_scales[:],
            in_=z_grouped[:].rearrange("p t x j -> p (t x j)"),
        )

        bias_ps = psum.tile([P, STEP], F32, tag="phi_ps")
        nc.tensor.matmul(out=bias_ps[:, 0:D], lhsT=ones[:], rhs=bias_rows[:, D : 2 * D], start=True, stop=True)
        for m in range(D_TILES):
            nc.tensor.matmul(
                out=bias_ps[:, D + 32 * m : D + 32 * (m + 1)],
                lhsT=bias_rows[:, P * m : P * (m + 1)],
                rhs=ones[:, 0:32],
                start=True,
                stop=True,
            )
        bg_sb = keep.tile([P, D], F32)
        nc.vector.tensor_copy(out=bg_sb[:], in_=bias_ps[:, 0:D])
        bp_sb = keep.tile([P, D_TILES], F32)
        nc.vector.tensor_copy(
            out=bp_sb[:], in_=bias_ps[:, D : D + 32 * D_TILES].rearrange("p (m x) -> p m x", x=32)[:, :, 0]
        )

        z_ps = psum.tile([P, D_TILES, D], F32, tag="g_ps")
        for m in range(D_TILES):
            nc.tensor.matmul_mx(
                out=z_ps[:, m, 0 : T * Z_REP],
                lhsT=wp_words[:, 1, P * m : P * (m + 1)].bitcast(FP8X4),
                lhsT_scale=wp_scales[:, 1, P * m : P * (m + 1)],
                rhs=z_words[:].bitcast(FP8X4),
                rhs_scale=z_scales[:],
                start=True,
                stop=True,
            )

        zz_words = keep.tile([P, T, P // 2], U32, align_bytes=64)
        nc.vector.tensor_copy(
            out=zz_words[:].bitcast(I32),
            in_=z_words[:].bitcast(I32).rearrange("p (t x) -> p t x", x=Z_REP)[:, :, 0:1].to_broadcast([P, T, P // 2]),
        )
        zz_scales = keep.tile([P, T, P // 2], U8, align_bytes=64)
        nc.vector.tensor_copy(
            out=zz_scales[:].bitcast(I32),
            in_=z_scales[:].bitcast(I32).unsqueeze(2).to_broadcast([P, T, P // 8]),
        )

        phi_bias = keep.tile([P, D_TILES, T], F32)
        for m in range(D_TILES):
            nc.vector.tensor_scalar(
                out=phi_bias[:, m, :],
                in0=z_ps[:, m, 0 : T * Z_REP].rearrange("p (t x) -> p t x", x=Z_REP)[:, :, 0],
                scalar1=bp_sb[:, m : m + 1],
                scalar2=None,
                op0=ADD,
            )

        grouped_of = {}
        packed_of = {}
        g_st_of = {}
        phi_st_of = {}
        group_of = {}
        group_first = 0
        for size in PHI_GROUPS:
            for s in range(group_first, group_first + size):
                group_of[s] = (group_first, size)
            group_first += size

        def regroup(e):
            s, h = divmod(e, 2)
            a_c, begin = a_of[s]
            columns = a_c[:, :, begin : begin + DOUBLE].rearrange("p j (q h r) -> p h q j r", h=2, r=ROWS)
            grouped = stage.tile([P, ROWS, P, PACK], BF16, align_bytes=64)
            regions = grouped[:].rearrange("p r q j -> p q j r")
            nc.vector.tensor_copy(out=regions[:, 0 : P // 2], in_=columns[:, h, 0 : P // 2])
            nc.scalar.copy(out=regions[:, P // 2 : P], in_=columns[:, h, P // 2 : P])
            grouped_of[e] = grouped

        def quantise(e):
            words = stage.tile([P, ROWS, P], U32, align_bytes=64)
            scales = stage.tile([P, ROWS, P], U8, align_bytes=64)
            nc.vector.quantize_mx(
                out=words[:].rearrange("p r q -> p (r q)").bitcast(FP8X4),
                scales=scales[:].rearrange("p r q -> p (r q)"),
                in_=grouped_of[e][:].rearrange("p r q j -> p (r q j)"),
            )
            packed_of[e] = (words, scales)

        def multiply_and_store(e):
            s, h = divmod(e, 2)
            words, scales = packed_of[e]
            group_s, size = group_of[s]
            first = (s - group_s) * DOUBLE
            for m in range(D_TILES):
                if first == 0 and h == 0 and m == 0:
                    phi_st_of[0] = outs.tile([P, D_TILES, size * DOUBLE], F32, name="phi_st", align_bytes=256)
                phi_st = phi_st_of[0]
                phi_ps = psum.tile([P, STEP], F32, tag="phi_ps")
                nc.tensor.matmul_mx(
                    out=phi_ps[:],
                    lhsT=wp_words[:, 0, P * m : P * (m + 1)].bitcast(FP8X4),
                    lhsT_scale=wp_scales[:, 0, P * m : P * (m + 1)],
                    rhs=words[:].rearrange("p r q -> p (r q)").bitcast(FP8X4),
                    rhs_scale=scales[:].rearrange("p r q -> p (r q)"),
                    start=True,
                    stop=True,
                )
                target = phi_st[:, m, first : first + DOUBLE].rearrange("d (q h r) -> d h q r", h=2, r=ROWS)
                source = phi_ps[:].rearrange("d (r q) -> d q r", r=ROWS)
                for w in range(2):
                    nc.scalar.activation(
                        out=target[:, h, (P // 2) * w : (P // 2) * (w + 1), :],
                        in_=source[:, (P // 2) * w : (P // 2) * (w + 1), :],
                        func=ACT.Identity,
                        bias=phi_bias[:, m, 2 * s + w : 2 * s + w + 1],
                        scale=1.0,
                    )
            if first == (size - 1) * DOUBLE and h == 1:
                nc.sync.dma_start(out=phi_rows[:, :, group_s * DOUBLE : (s + 1) * DOUBLE], in_=phi_st_of[0][:])

            if h == 0:
                g_st_of[0] = outs.tile([P, 2 * ROWS, D], F32, name="g_st", align_bytes=256)
            g_st = g_st_of[0]
            for r0 in range(0, ROWS, 2):
                g_ps = psum.tile([P, 2, D], F32, tag="g_ps")
                for i in range(2):
                    nc.tensor.matmul_mx(
                        out=g_ps[:, i, :],
                        lhsT=words[:, r0 + i, :].bitcast(FP8X4),
                        lhsT_scale=scales[:, r0 + i, :],
                        rhs=wg_words[:, 0, :].bitcast(FP8X4),
                        rhs_scale=wg_scales[:, 0, :],
                        start=True,
                        stop=False,
                    )
                    nc.tensor.matmul_mx(
                        out=g_ps[:, i, :],
                        lhsT=zz_words[:, 2 * s : 2 * s + 2, :].rearrange("p t q -> p (t q)").bitcast(FP8X4),
                        lhsT_scale=zz_scales[:, 2 * s : 2 * s + 2, :].rearrange("p t q -> p (t q)"),
                        rhs=wg_words[:, 1, :].bitcast(FP8X4),
                        rhs_scale=wg_scales[:, 1, :],
                        start=False,
                        stop=True,
                    )
                nc.vector.tensor_tensor(
                    out=g_st[:, ROWS * h + r0 : ROWS * h + r0 + 2, :],
                    in0=g_ps[:],
                    in1=bg_sb[:].unsqueeze(1).to_broadcast([P, 2, D]),
                    op=ADD,
                )
            if s == UNITS // 2 - 1:
                nc.sync.dma_start(
                    out=g_halves[s, h], in_=g_st[:, ROWS * h : ROWS * (h + 1), :].rearrange("q r d -> q (r d)")
                )
            elif h == 1:
                nc.sync.dma_start(out=g_rows[s], in_=g_st[:].rearrange("q r d -> q (r d)"))

        regroup(0)
        regroup(1)
        quantise(0)
        for e in range(UNITS):
            if e + 2 < UNITS:
                regroup(e + 2)
            if e + 1 < UNITS:
                quantise(e + 1)
            multiply_and_store(e)
